import numpy as np
import ml_dtypes


def mxq(x, axis, fmt="e4m3"):
    dtype, down = {"e4m3": (ml_dtypes.float8_e4m3fn, 7), "e5m2": (ml_dtypes.float8_e5m2, 14)}[fmt]
    v = np.moveaxis(np.asarray(x, np.float32).astype(ml_dtypes.bfloat16).astype(np.float64), axis, -1)
    blocks = v.reshape(v.shape[:-1] + (-1, 32))
    amax = np.abs(blocks).max(-1, keepdims=True)
    byte = np.maximum(np.where(amax > 0, np.frexp(amax)[1] - 1 + 127, 0) - down, 1)
    scale = np.exp2(byte - 127.0)
    codes = (blocks / scale).astype(np.float32).astype(dtype).astype(np.float64)
    return np.moveaxis((codes * scale).reshape(v.shape), -1, axis)


WIDE = False


def mx_kscale(k):
    if not WIDE:
        return np.ones(k)
    levels = np.array([10, -10, 5, -5, 0])
    a = np.random.permutation(np.resize(levels, k // 512 * 4)).reshape(k // 512, 4)
    idx = np.arange(k)
    return np.exp2(a[idx // 512, idx % 128 // 32])


BF16 = ml_dtypes.bfloat16


def bf(x):
    return np.asarray(x, np.float32).astype(BF16)


def f64(x):
    return np.asarray(x).astype(np.float64)


B, DIN, DOUT, ORDER = 2048, 1024, 1024, 8


def householder_cols(v):
    vn = v / np.sqrt(np.sum(v * v))
    return np.eye(DIN)[:, :DOUT] - 2.0 * vn[:, None] * vn[None, :DOUT]


def setup_inputs():
    s = mx_kscale(DIN)
    return {"x": bf(np.random.standard_normal((B, DIN)) * s),
            "u_prev": bf(np.random.standard_normal((DIN, DIN)) / np.sqrt(DIN) / s[:, None]),
            "v_last": bf(np.random.standard_normal(DIN)),
            "d": bf(np.random.standard_normal(DOUT)),
            "bias": bf(np.random.standard_normal(DOUT) * 0.3)}


def reference(x, u_prev, v_last, d, bias):
    h = householder_cols(f64(v_last))
    u = mxq(f64(u_prev), 1, "e4m3") @ mxq(h, 0, "e4m3")
    w = u * f64(d)[None, :]
    return (mxq(f64(x), 1, "e4m3") @ mxq(w, 0, "e4m3")) + f64(bias)[None, :]

@@ -1,0 +1,221 @@
+from contextlib import ExitStack
+
+import concourse.mybir as mybir
+from concourse.masks import make_identity
+
+FP8X4 = mybir.dt.float8_e4m3fn_x4
+BF16 = mybir.dt.bfloat16
+F32 = mybir.dt.float32
+U32 = mybir.dt.uint32
+U8 = mybir.dt.uint8
+ALU = mybir.AluOpType
+ACT = mybir.ActivationFunctionType
+
+B, DIN, DOUT = 2048, 1024, 1024
+FLOPS = 2 * DIN * DIN * DOUT + 2 * B * DIN * DOUT
+
+P = 128
+PACK = 4
+K_PASS = P * PACK
+PASSES = DIN // K_PASS
+CHUNK = 2 * P
+U_CHUNKS = DIN // CHUNK
+X_CHUNKS = B // CHUNK
+BLOCKS = DOUT // P
+N_WIDE = 512
+SWEEPS = DOUT // N_WIDE
+BLOCKS_PER_SWEEP = BLOCKS // SWEEPS
+
+
+def tile_orthogonaldense_pb_kernel(tc, x, u_prev, v_last, d, bias, out):
+    nc = tc.nc
+    with ExitStack() as stack:
+        const = stack.enter_context(tc.tile_pool(name="const", bufs=1))
+        rows_pool = stack.enter_context(tc.tile_pool(name="rows", bufs=U_CHUNKS + X_CHUNKS))
+        stage = stack.enter_context(tc.tile_pool(name="stage", bufs=4))
+        keep = stack.enter_context(tc.tile_pool(name="keep", bufs=1))
+        y_pool = stack.enter_context(tc.tile_pool(name="y", bufs=8))
+        psum = stack.enter_context(tc.psum_pool(name="psum", bufs=8))
+
+        v_bc = const.tile([P, DIN], BF16)
+        nc.scalar.dma_start(out=v_bc[:], in_=v_last.partition_broadcast(P))
+        u_rows = []
+        for a in range(U_CHUNKS):
+            rows = rows_pool.tile([P, 2, DIN], BF16, tag="rows")
+            nc.sync.dma_start(
+                out=rows[:],
+                in_=u_prev[a * CHUNK : (a + 1) * CHUNK, :].rearrange("(p r) k -> p r k", r=2),
+            )
+            u_rows.append(rows)
+        d_bc = const.tile([P, DOUT], BF16)
+        nc.sync.dma_start(out=d_bc[:], in_=d.partition_broadcast(P))
+        x_rows = []
+        for c in range(X_CHUNKS):
+            rows = rows_pool.tile([P, 2, DIN], BF16, tag="rows")
+            nc.sync.dma_start(
+                out=rows[:],
+                in_=x[c * CHUNK : (c + 1) * CHUNK, :].rearrange("(p r) k -> p r k", r=2),
+            )
+            x_rows.append(rows)
+        bias_bc = const.tile([P, DOUT], BF16)
+        nc.sync.dma_start(out=bias_bc[:], in_=bias.partition_broadcast(P))
+
+        ident = const.tile([P, P], F32)
+        make_identity(nc, ident[:])
+        eye = const.tile([P, K_PASS, PACK], BF16)
+        nc.vector.memset(eye[:], 0.0)
+        nc.gpsimd.affine_select(
+            out=eye[:],
+            in_=eye[:],
+            compare_op=ALU.not_equal,
+            fill=1.0,
+            base=0,
+            pattern=[[1, K_PASS], [-2 * P, 2], [-1, 2]],
+            channel_multiplier=-2,
+        )
+
+        u_codes = keep.tile([P, U_CHUNKS, PASSES, CHUNK], U32, align_bytes=64)
+        u_scales = keep.tile([P, U_CHUNKS, PASSES, CHUNK], U8, align_bytes=64)
+        x_codes = keep.tile([P, X_CHUNKS, PASSES, CHUNK], U32, align_bytes=64)
+        x_scales = keep.tile([P, X_CHUNKS, PASSES, CHUNK], U8, align_bytes=64)
+        h_codes = keep.tile([P, BLOCKS, PASSES, P], U32, align_bytes=64)
+        h_scales = keep.tile([P, BLOCKS, PASSES, P], U8, align_bytes=64)
+        w_codes = keep.tile([P, PASSES, DOUT], U32, align_bytes=64)
+        w_scales = keep.tile([P, PASSES, DOUT], U8, align_bytes=64)
+
+        def rows_to_codes(rows, codes, scales):
+            words = rows[:].rearrange("p r k -> p (r k)").bitcast(F32)
+            words = words.rearrange("p (r w) -> p r w", r=2)
+            grouped = stage.tile([P, PASSES, CHUNK, PACK], BF16, align_bytes=64)
+            grouped_words = grouped[:].rearrange("p g c t -> p (g c t)").bitcast(F32)
+            grouped_words = grouped_words.rearrange("p (g c u) -> p g c u", g=PASSES, u=2)
+            for g in range(PASSES):
+                bank = psum.tile([P, 2, CHUNK], F32, tag="bank")
+                for u in range(2):
+                    first = (2 * g + u) * P
+                    for r in range(2):
+                        nc.tensor.transpose(
+                            bank[:, u, r * P : (r + 1) * P], words[:, r, first : first + P], ident[:]
+                        )
+                nc.scalar.copy(out=grouped_words[:, g], in_=bank[:].rearrange("p u c -> p c u"))
+            nc.vector.quantize_mx(
+                out=codes.rearrange("p g c -> p (g c)").bitcast(FP8X4),
+                scales=scales.rearrange("p g c -> p (g c)"),
+                in_=grouped[:].rearrange("p g c t -> p (g c t)"),
+            )
+
+        squares = const.tile([P, DIN], BF16)
+        sum_squares = const.tile([P, 1], F32)
+        nc.scalar.activation(out=squares[:], in_=v_bc[:], func=ACT.Square, accum_out=sum_squares[:])
+        denominator = const.tile([P, 1], F32)
+        nc.vector.tensor_scalar_mul(out=denominator[:], in0=sum_squares[:], scalar1=-0.5 * P)
+        factor = const.tile([P, 1], F32)
+        nc.vector.reciprocal(out=factor[:], in_=denominator[:])
+        v_by_word = v_bc[:].rearrange("p (g u m e) -> p g u e m", g=PASSES, u=2, e=2)
+
+        def h_block(block):
+            cols = slice(block * P, (block + 1) * P)
+            h_grouped = stage.tile([P, PASSES, P, PACK], BF16, align_bytes=64)
+            for g in range(PASSES):
+                bank = psum.tile([P, PACK, P], F32, tag="bank")
+                for t in range(PACK):
+                    nc.tensor.matmul(
+                        out=bank[:, t, :],
+                        lhsT=v_by_word[:, g, t // 2, t % 2, :],
+                        rhs=v_bc[:, cols],
+                        start=True,
+                        stop=True,
+                    )
+                products = bank[:].rearrange("p t j -> p j t")
+                if g == block // BLOCKS_PER_SWEEP:
+                    first = (block % BLOCKS_PER_SWEEP) * P
+                    nc.vector.scalar_tensor_tensor(
+                        out=h_grouped[:, g],
+                        in0=products,
+                        scalar=factor[:, 0:1],
+                        in1=eye[:, first : first + P, :],
+                        op0=ALU.mult,
+                        op1=ALU.add,
+                    )
+                else:
+                    nc.scalar.activation(
+                        out=h_grouped[:, g], in_=products, func=ACT.Copy, scale=factor[:, 0:1]
+                    )
+            nc.vector.quantize_mx(
+                out=h_codes[:, block].rearrange("p g j -> p (g j)").bitcast(FP8X4),
+                scales=h_scales[:, block].rearrange("p g j -> p (g j)"),
+                in_=h_grouped[:].rearrange("p g j t -> p (g j t)"),
+            )
+
+        def w_block(block):
+            cols = slice(block * P, (block + 1) * P)
+            for gi in range(PASSES):
+                bank = psum.tile([P, PACK, P], F32, tag="bank")
+                for t in range(PACK):
+                    chunk = 2 * gi + t // 2
+                    rows_e = slice((t % 2) * P, (t % 2 + 1) * P)
+                    for g in range(PASSES):
+                        nc.tensor.matmul_mx(
+                            out=bank[:, t, :],
+                            lhsT=u_codes[:, chunk, g, rows_e].bitcast(FP8X4),
+                            lhsT_scale=u_scales[:, chunk, g, rows_e],
+                            rhs=h_codes[:, block, g, :].bitcast(FP8X4),
+                            rhs_scale=h_scales[:, block, g, :],
+                            start=(g == 0),
+                            stop=(g == PASSES - 1),
+                        )
+                w_grouped = stage.tile([P, P, PACK], BF16, align_bytes=64)
+                nc.vector.tensor_tensor(
+                    out=w_grouped[:],
+                    in0=bank[:].rearrange("p t j -> p j t"),
+                    in1=d_bc[:, cols].unsqueeze(2).to_broadcast([P, P, PACK]),
+                    op=ALU.mult,
+                )
+                nc.vector.quantize_mx(
+                    out=w_codes[:, gi, cols].bitcast(FP8X4),
+                    scales=w_scales[:, gi, cols],
+                    in_=w_grouped[:].rearrange("p j t -> p (j t)"),
+                )
+
+        def y_bank(sweep, c, r):
+            cols = slice(sweep * N_WIDE, (sweep + 1) * N_WIDE)
+            rows_r = slice(r * P, (r + 1) * P)
+            bank = psum.tile([P, N_WIDE], F32, tag="bank")
+            for g in range(PASSES):
+                nc.tensor.matmul_mx(
+                    out=bank[:],
+                    lhsT=x_codes[:, c, g, rows_r].bitcast(FP8X4),
+                    lhsT_scale=x_scales[:, c, g, rows_r],
+                    rhs=w_codes[:, g, cols].bitcast(FP8X4),
+                    rhs_scale=w_scales[:, g, cols],
+                    start=(g == 0),
+                    stop=(g == PASSES - 1),
+                )
+            y_sb = y_pool.tile([P, N_WIDE], F32)
+            if (2 * c + r) % 3 == 2:
+                nc.scalar.copy(out=y_sb[:], in_=bank[:])
+                nc.gpsimd.tensor_tensor(out=y_sb[:], in0=y_sb[:], in1=bias_bc[:, cols], op=ALU.add)
+            else:
+                nc.vector.tensor_tensor(out=y_sb[:], in0=bank[:], in1=bias_bc[:, cols], op=ALU.add)
+            y_rows = out[c * CHUNK : (c + 1) * CHUNK, :].rearrange("(p r) j -> p r j", r=2)
+            nc.sync.dma_start(out=y_rows[:, r, cols], in_=y_sb[:])
+
+        for a in range(U_CHUNKS):
+            rows_to_codes(u_rows[a], u_codes[:, a], u_scales[:, a])
+        h_block(0)
+        for block in range(BLOCKS_PER_SWEEP):
+            h_block(block + 1)
+            w_block(block)
+            for c in (2 * block, 2 * block + 1):
+                rows_to_codes(x_rows[c], x_codes[:, c], x_scales[:, c])
+        for c in range(X_CHUNKS):
+            for r in range(2):
+                y_bank(0, c, r)
+            if c % 2 == 1:
+                block = BLOCKS_PER_SWEEP + c // 2
+                if block + 1 < BLOCKS:
+                    h_block(block + 1)
+                w_block(block)
+        for c in range(X_CHUNKS):
+            for r in range(2):
+                y_bank(1, c, r)

@@ -36,6 +36,7 @@ def tile_orthogonaldense_pb_kernel(tc, x, u_prev, v_last, d, bias, out):
         keep = stack.enter_context(tc.tile_pool(name="keep", bufs=1))
         y_pool = stack.enter_context(tc.tile_pool(name="y", bufs=8))
         psum = stack.enter_context(tc.psum_pool(name="psum", bufs=8))
+        stack.enter_context(tc.manual_schedule())
 
         v_bc = const.tile([P, DIN], BF16)
         nc.scalar.dma_start(out=v_bc[:], in_=v_last.partition_broadcast(P))
@@ -62,17 +63,12 @@ def tile_orthogonaldense_pb_kernel(tc, x, u_prev, v_last, d, bias, out):
 
         ident = const.tile([P, P], F32)
         make_identity(nc, ident[:])
-        eye = const.tile([P, K_PASS, PACK], BF16)
+        eye = const.tile([P, 2, P, 2, PACK], BF16)
         nc.vector.memset(eye[:], 0.0)
-        nc.gpsimd.affine_select(
-            out=eye[:],
-            in_=eye[:],
-            compare_op=ALU.not_equal,
-            fill=1.0,
-            base=0,
-            pattern=[[1, K_PASS], [-2 * P, 2], [-1, 2]],
-            channel_multiplier=-2,
-        )
+        for u in range(2):
+            for e in range(2):
+                nc.vector.tensor_copy(out=eye[:, u, :, e, 2 * u + e], in_=ident[:])
+        eye_cols = eye[:].rearrange("p u q e t -> p (u q e) t")
 
         u_codes = keep.tile([P, U_CHUNKS, PASSES, CHUNK], U32, align_bytes=64)
         u_scales = keep.tile([P, U_CHUNKS, PASSES, CHUNK], U8, align_bytes=64)
@@ -83,7 +79,7 @@ def tile_orthogonaldense_pb_kernel(tc, x, u_prev, v_last, d, bias, out):
         w_codes = keep.tile([P, PASSES, DOUT], U32, align_bytes=64)
         w_scales = keep.tile([P, PASSES, DOUT], U8, align_bytes=64)
 
-        def rows_to_codes(rows, codes, scales):
+        def transpose_rows(rows):
             words = rows[:].rearrange("p r k -> p (r k)").bitcast(F32)
             words = words.rearrange("p (r w) -> p r w", r=2)
             grouped = stage.tile([P, PASSES, CHUNK, PACK], BF16, align_bytes=64)
@@ -98,22 +94,30 @@ def tile_orthogonaldense_pb_kernel(tc, x, u_prev, v_last, d, bias, out):
                             bank[:, u, r * P : (r + 1) * P], words[:, r, first : first + P], ident[:]
                         )
                 nc.scalar.copy(out=grouped_words[:, g], in_=bank[:].rearrange("p u c -> p c u"))
+            return grouped
+
+        def quantise_rows(grouped, codes, scales):
             nc.vector.quantize_mx(
                 out=codes.rearrange("p g c -> p (g c)").bitcast(FP8X4),
                 scales=scales.rearrange("p g c -> p (g c)"),
                 in_=grouped[:].rearrange("p g c t -> p (g c t)"),
             )
 
-        squares = const.tile([P, DIN], BF16)
-        sum_squares = const.tile([P, 1], F32)
-        nc.scalar.activation(out=squares[:], in_=v_bc[:], func=ACT.Square, accum_out=sum_squares[:])
-        denominator = const.tile([P, 1], F32)
-        nc.vector.tensor_scalar_mul(out=denominator[:], in0=sum_squares[:], scalar1=-0.5 * P)
         factor = const.tile([P, 1], F32)
-        nc.vector.reciprocal(out=factor[:], in_=denominator[:])
+
+        def reflection_factor():
+            squares = const.tile([P, DIN], BF16)
+            sum_squares = const.tile([P, 1], F32)
+            nc.scalar.activation(
+                out=squares[:], in_=v_bc[:], func=ACT.Square, accum_out=sum_squares[:]
+            )
+            denominator = const.tile([P, 1], F32)
+            nc.vector.tensor_scalar_mul(out=denominator[:], in0=sum_squares[:], scalar1=-0.5 * P)
+            nc.vector.reciprocal(out=factor[:], in_=denominator[:])
+
         v_by_word = v_bc[:].rearrange("p (g u m e) -> p g u e m", g=PASSES, u=2, e=2)
 
-        def h_block(block):
+        def h_products(block):
             cols = slice(block * P, (block + 1) * P)
             h_grouped = stage.tile([P, PASSES, P, PACK], BF16, align_bytes=64)
             for g in range(PASSES):
@@ -133,7 +137,7 @@ def tile_orthogonaldense_pb_kernel(tc, x, u_prev, v_last, d, bias, out):
                         out=h_grouped[:, g],
                         in0=products,
                         scalar=factor[:, 0:1],
-                        in1=eye[:, first : first + P, :],
+                        in1=eye_cols[:, first : first + P, :],
                         op0=ALU.mult,
                         op1=ALU.add,
                     )
@@ -141,14 +145,18 @@ def tile_orthogonaldense_pb_kernel(tc, x, u_prev, v_last, d, bias, out):
                     nc.scalar.activation(
                         out=h_grouped[:, g], in_=products, func=ACT.Copy, scale=factor[:, 0:1]
                     )
+            return h_grouped
+
+        def quantise_h(block, h_grouped):
             nc.vector.quantize_mx(
                 out=h_codes[:, block].rearrange("p g j -> p (g j)").bitcast(FP8X4),
                 scales=h_scales[:, block].rearrange("p g j -> p (g j)"),
                 in_=h_grouped[:].rearrange("p g j t -> p (g j t)"),
             )
 
-        def w_block(block):
+        def w_products(block):
             cols = slice(block * P, (block + 1) * P)
+            w_grouped = stage.tile([P, PASSES, P, PACK], BF16, align_bytes=64)
             for gi in range(PASSES):
                 bank = psum.tile([P, PACK, P], F32, tag="bank")
                 for t in range(PACK):
@@ -164,17 +172,21 @@ def tile_orthogonaldense_pb_kernel(tc, x, u_prev, v_last, d, bias, out):
                             start=(g == 0),
                             stop=(g == PASSES - 1),
                         )
-                w_grouped = stage.tile([P, P, PACK], BF16, align_bytes=64)
                 nc.vector.tensor_tensor(
-                    out=w_grouped[:],
+                    out=w_grouped[:, gi],
                     in0=bank[:].rearrange("p t j -> p j t"),
                     in1=d_bc[:, cols].unsqueeze(2).to_broadcast([P, P, PACK]),
                     op=ALU.mult,
                 )
+            return w_grouped
+
+        def quantise_w(block, w_grouped):
+            cols = slice(block * P, (block + 1) * P)
+            for gi in range(PASSES):
                 nc.vector.quantize_mx(
                     out=w_codes[:, gi, cols].bitcast(FP8X4),
                     scales=w_scales[:, gi, cols],
-                    in_=w_grouped[:].rearrange("p j t -> p (j t)"),
+                    in_=w_grouped[:, gi].rearrange("p j t -> p (j t)"),
                 )
 
         def y_bank(sweep, c, r):
@@ -192,7 +204,7 @@ def tile_orthogonaldense_pb_kernel(tc, x, u_prev, v_last, d, bias, out):
                     stop=(g == PASSES - 1),
                 )
             y_sb = y_pool.tile([P, N_WIDE], F32)
-            if (2 * c + r) % 3 == 2:
+            if (2 * c + r) % 3 == 1:
                 nc.scalar.copy(out=y_sb[:], in_=bank[:])
                 nc.gpsimd.tensor_tensor(out=y_sb[:], in0=y_sb[:], in1=bias_bc[:, cols], op=ALU.add)
             else:
@@ -200,22 +212,39 @@ def tile_orthogonaldense_pb_kernel(tc, x, u_prev, v_last, d, bias, out):
             y_rows = out[c * CHUNK : (c + 1) * CHUNK, :].rearrange("(p r) j -> p r j", r=2)
             nc.sync.dma_start(out=y_rows[:, r, cols], in_=y_sb[:])
 
-        for a in range(U_CHUNKS):
-            rows_to_codes(u_rows[a], u_codes[:, a], u_scales[:, a])
-        h_block(0)
+
+        u_grouped = [transpose_rows(u_rows[0])]
+        for a in range(1, U_CHUNKS):
+            u_grouped.append(transpose_rows(u_rows[a]))
+            quantise_rows(u_grouped[a - 1], u_codes[:, a - 1], u_scales[:, a - 1])
+            if a == 1:
+                reflection_factor()
+        h_grouped = h_products(0)
+        quantise_rows(u_grouped[U_CHUNKS - 1], u_codes[:, U_CHUNKS - 1], u_scales[:, U_CHUNKS - 1])
+        quantise_h(0, h_grouped)
+
         for block in range(BLOCKS_PER_SWEEP):
-            h_block(block + 1)
-            w_block(block)
-            for c in (2 * block, 2 * block + 1):
-                rows_to_codes(x_rows[c], x_codes[:, c], x_scales[:, c])
+            h_grouped = h_products(block + 1)
+            w_grouped = w_products(block)
+            x_grouped = [transpose_rows(x_rows[2 * block + i]) for i in range(2)]
+            quantise_w(block, w_grouped)
+            quantise_h(block + 1, h_grouped)
+            for i in range(2):
+                c = 2 * block + i
+                quantise_rows(x_grouped[i], x_codes[:, c], x_scales[:, c])
+
         for c in range(X_CHUNKS):
             for r in range(2):
                 y_bank(0, c, r)
-            if c % 2 == 1:
+            if c % 2 == 0:
                 block = BLOCKS_PER_SWEEP + c // 2
                 if block + 1 < BLOCKS:
-                    h_block(block + 1)
-                w_block(block)
+                    h_grouped = h_products(block + 1)
+                w_grouped = w_products(block)
+                quantise_w(block, w_grouped)
+                if block + 1 < BLOCKS:
+                    quantise_h(block + 1, h_grouped)
+
         for c in range(X_CHUNKS):
             for r in range(2):
                 y_bank(1, c, r)

@@ -38,8 +38,17 @@ def tile_orthogonaldense_pb_kernel(tc, x, u_prev, v_last, d, bias, out):
         psum = stack.enter_context(tc.psum_pool(name="psum", bufs=8))
         stack.enter_context(tc.manual_schedule())
 
-        v_bc = const.tile([P, DIN], BF16)
-        nc.scalar.dma_start(out=v_bc[:], in_=v_last.partition_broadcast(P))
+        v_col = const.tile([P, DIN // P], BF16)
+        nc.scalar.dma_start(out=v_col[:], in_=v_last.rearrange("(p c) -> p c", p=P))
+        v_row = const.tile([P, DIN], BF16)
+        nc.vector.memset(v_row[:], 0.0)
+        nc.scalar.dma_start(out=v_row[0:1, :], in_=v_last.rearrange("(o k) -> o k", o=1))
+        d_row = const.tile([P, DOUT], BF16)
+        nc.vector.memset(d_row[:], 0.0)
+        nc.scalar.dma_start(out=d_row[0:1, :], in_=d.rearrange("(o j) -> o j", o=1))
+        bias_row = const.tile([P, DOUT], BF16)
+        nc.vector.memset(bias_row[:], 0.0)
+        nc.scalar.dma_start(out=bias_row[0:1, :], in_=bias.rearrange("(o j) -> o j", o=1))
         u_rows = []
         for a in range(U_CHUNKS):
             rows = rows_pool.tile([P, 2, DIN], BF16, tag="rows")
@@ -48,8 +57,6 @@ def tile_orthogonaldense_pb_kernel(tc, x, u_prev, v_last, d, bias, out):
                 in_=u_prev[a * CHUNK : (a + 1) * CHUNK, :].rearrange("(p r) k -> p r k", r=2),
             )
             u_rows.append(rows)
-        d_bc = const.tile([P, DOUT], BF16)
-        nc.sync.dma_start(out=d_bc[:], in_=d.partition_broadcast(P))
         x_rows = []
         for c in range(X_CHUNKS):
             rows = rows_pool.tile([P, 2, DIN], BF16, tag="rows")
@@ -58,9 +65,11 @@ def tile_orthogonaldense_pb_kernel(tc, x, u_prev, v_last, d, bias, out):
                 in_=x[c * CHUNK : (c + 1) * CHUNK, :].rearrange("(p r) k -> p r k", r=2),
             )
             x_rows.append(rows)
-        bias_bc = const.tile([P, DOUT], BF16)
-        nc.sync.dma_start(out=bias_bc[:], in_=bias.partition_broadcast(P))
 
+        ones_f32 = const.tile([P, P], F32)
+        nc.vector.memset(ones_f32[:], 1.0)
+        ones_bf16 = const.tile([P, P], BF16)
+        nc.vector.memset(ones_bf16[:], 1.0)
         ident = const.tile([P, P], F32)
         make_identity(nc, ident[:])
         eye = const.tile([P, 2, P, 2, PACK], BF16)
@@ -106,16 +115,25 @@ def tile_orthogonaldense_pb_kernel(tc, x, u_prev, v_last, d, bias, out):
         factor = const.tile([P, 1], F32)
 
         def reflection_factor():
-            squares = const.tile([P, DIN], BF16)
-            sum_squares = const.tile([P, 1], F32)
-            nc.scalar.activation(
-                out=squares[:], in_=v_bc[:], func=ACT.Square, accum_out=sum_squares[:]
-            )
+            squares = const.tile([P, DIN // P], F32)
+            partial = const.tile([P, 1], F32)
+            nc.scalar.activation(out=squares[:], in_=v_col[:], func=ACT.Square, accum_out=partial[:])
+            total = psum.tile([P, 1], F32, tag="bank")
+            nc.tensor.matmul(out=total[:], lhsT=ones_f32[:], rhs=partial[:], start=True, stop=True)
             denominator = const.tile([P, 1], F32)
-            nc.vector.tensor_scalar_mul(out=denominator[:], in0=sum_squares[:], scalar1=-0.5 * P)
+            nc.vector.tensor_scalar_mul(out=denominator[:], in0=total[:], scalar1=-0.5)
             nc.vector.reciprocal(out=factor[:], in_=denominator[:])
 
-        v_by_word = v_bc[:].rearrange("p (g u m e) -> p g u e m", g=PASSES, u=2, e=2)
+        def spread(row, everywhere):
+            bank = psum.tile([P, DOUT], BF16, tag="bank")
+            for half in range(DOUT // N_WIDE):
+                cols = slice(half * N_WIDE, (half + 1) * N_WIDE)
+                nc.tensor.matmul(
+                    out=bank[:, cols], lhsT=ones_bf16[:], rhs=row[:, cols], start=True, stop=True
+                )
+            nc.scalar.copy(out=everywhere[:], in_=bank[:])
+
+        v_by_word = v_row[:].rearrange("p (g u m e) -> p g u e m", g=PASSES, u=2, e=2)
 
         def h_products(block):
             cols = slice(block * P, (block + 1) * P)
@@ -126,7 +144,7 @@ def tile_orthogonaldense_pb_kernel(tc, x, u_prev, v_last, d, bias, out):
                     nc.tensor.matmul(
                         out=bank[:, t, :],
                         lhsT=v_by_word[:, g, t // 2, t % 2, :],
-                        rhs=v_bc[:, cols],
+                        rhs=v_row[:, cols],
                         start=True,
                         stop=True,
                     )
@@ -213,12 +231,16 @@ def tile_orthogonaldense_pb_kernel(tc, x, u_prev, v_last, d, bias, out):
             nc.sync.dma_start(out=y_rows[:, r, cols], in_=y_sb[:])
 
 
+        reflection_factor()
+        d_bc = const.tile([P, DOUT], BF16)
+        spread(d_row, d_bc)
+        bias_bc = const.tile([P, DOUT], BF16)
+        spread(bias_row, bias_bc)
+
         u_grouped = [transpose_rows(u_rows[0])]
         for a in range(1, U_CHUNKS):
             u_grouped.append(transpose_rows(u_rows[a]))
             quantise_rows(u_grouped[a - 1], u_codes[:, a - 1], u_scales[:, a - 1])
-            if a == 1:
-                reflection_factor()
         h_grouped = h_products(0)
         quantise_rows(u_grouped[U_CHUNKS - 1], u_codes[:, U_CHUNKS - 1], u_scales[:, U_CHUNKS - 1])
         quantise_h(0, h_grouped)

@@ -8,6 +8,7 @@ BF16 = mybir.dt.bfloat16
 F32 = mybir.dt.float32
 U32 = mybir.dt.uint32
 U8 = mybir.dt.uint8
+I32 = mybir.dt.int32
 ALU = mybir.AluOpType
 ACT = mybir.ActivationFunctionType
 
@@ -25,6 +26,7 @@ BLOCKS = DOUT // P
 N_WIDE = 512
 SWEEPS = DOUT // N_WIDE
 BLOCKS_PER_SWEEP = BLOCKS // SWEEPS
+assert U_CHUNKS == BLOCKS_PER_SWEEP and X_CHUNKS == 2 * BLOCKS_PER_SWEEP
 
 
 def tile_orthogonaldense_pb_kernel(tc, x, u_prev, v_last, d, bias, out):
@@ -41,13 +43,17 @@ def tile_orthogonaldense_pb_kernel(tc, x, u_prev, v_last, d, bias, out):
         v_col = const.tile([P, DIN // P], BF16)
         nc.scalar.dma_start(out=v_col[:], in_=v_last.rearrange("(p c) -> p c", p=P))
         v_row = const.tile([P, DIN], BF16)
-        nc.vector.memset(v_row[:], 0.0)
+        nc.vector.memset(v_row[:].bitcast(I32), 0)
         nc.scalar.dma_start(out=v_row[0:1, :], in_=v_last.rearrange("(o k) -> o k", o=1))
+        ones_f32 = const.tile([P, P], F32)
+        nc.vector.memset(ones_f32[:], 1.0)
+        warm = const.tile([P, 1], F32)
+        nc.scalar.activation(out=warm[:], in_=ones_f32[:, 0:1], func=ACT.Square)
         d_row = const.tile([P, DOUT], BF16)
-        nc.vector.memset(d_row[:], 0.0)
+        nc.vector.memset(d_row[:].bitcast(I32), 0)
         nc.scalar.dma_start(out=d_row[0:1, :], in_=d.rearrange("(o j) -> o j", o=1))
         bias_row = const.tile([P, DOUT], BF16)
-        nc.vector.memset(bias_row[:], 0.0)
+        nc.vector.memset(bias_row[:].bitcast(I32), 0)
         nc.scalar.dma_start(out=bias_row[0:1, :], in_=bias.rearrange("(o j) -> o j", o=1))
         u_rows = []
         for a in range(U_CHUNKS):
@@ -66,14 +72,12 @@ def tile_orthogonaldense_pb_kernel(tc, x, u_prev, v_last, d, bias, out):
             )
             x_rows.append(rows)
 
-        ones_f32 = const.tile([P, P], F32)
-        nc.vector.memset(ones_f32[:], 1.0)
         ones_bf16 = const.tile([P, P], BF16)
         nc.vector.memset(ones_bf16[:], 1.0)
         ident = const.tile([P, P], F32)
         make_identity(nc, ident[:])
         eye = const.tile([P, 2, P, 2, PACK], BF16)
-        nc.vector.memset(eye[:], 0.0)
+        nc.vector.memset(eye[:].rearrange("p u q e t -> p (u q e t)").bitcast(I32), 0)
         for u in range(2):
             for e in range(2):
                 nc.vector.tensor_copy(out=eye[:, u, :, e, 2 * u + e], in_=ident[:])
@@ -232,25 +236,29 @@ def tile_orthogonaldense_pb_kernel(tc, x, u_prev, v_last, d, bias, out):
 
 
         reflection_factor()
+        h_grouped = []
+        u_grouped = []
+        for a in range(U_CHUNKS):
+            h_grouped.append(h_products(a))
+            u_grouped.append(transpose_rows(u_rows[a]))
+            if a > 0:
+                quantise_h(a - 1, h_grouped[a - 1])
+                quantise_rows(u_grouped[a - 1], u_codes[:, a - 1], u_scales[:, a - 1])
+        last = U_CHUNKS - 1
+        quantise_h(last, h_grouped[last])
         d_bc = const.tile([P, DOUT], BF16)
         spread(d_row, d_bc)
+        quantise_rows(u_grouped[last], u_codes[:, last], u_scales[:, last])
         bias_bc = const.tile([P, DOUT], BF16)
         spread(bias_row, bias_bc)
 
-        u_grouped = [transpose_rows(u_rows[0])]
-        for a in range(1, U_CHUNKS):
-            u_grouped.append(transpose_rows(u_rows[a]))
-            quantise_rows(u_grouped[a - 1], u_codes[:, a - 1], u_scales[:, a - 1])
-        h_grouped = h_products(0)
-        quantise_rows(u_grouped[U_CHUNKS - 1], u_codes[:, U_CHUNKS - 1], u_scales[:, U_CHUNKS - 1])
-        quantise_h(0, h_grouped)
-
         for block in range(BLOCKS_PER_SWEEP):
-            h_grouped = h_products(block + 1)
+            later = block + BLOCKS_PER_SWEEP
+            h_later = h_products(later)
             w_grouped = w_products(block)
             x_grouped = [transpose_rows(x_rows[2 * block + i]) for i in range(2)]
             quantise_w(block, w_grouped)
-            quantise_h(block + 1, h_grouped)
+            quantise_h(later, h_later)
             for i in range(2):
                 c = 2 * block + i
                 quantise_rows(x_grouped[i], x_codes[:, c], x_scales[:, c])
@@ -260,12 +268,8 @@ def tile_orthogonaldense_pb_kernel(tc, x, u_prev, v_last, d, bias, out):
                 y_bank(0, c, r)
             if c % 2 == 0:
                 block = BLOCKS_PER_SWEEP + c // 2
-                if block + 1 < BLOCKS:
-                    h_grouped = h_products(block + 1)
                 w_grouped = w_products(block)
                 quantise_w(block, w_grouped)
-                if block + 1 < BLOCKS:
-                    quantise_h(block + 1, h_grouped)
 
         for c in range(X_CHUNKS):
             for r in range(2):

@@ -41,20 +41,10 @@ def tile_orthogonaldense_pb_kernel(tc, x, u_prev, v_last, d, bias, out):
         stack.enter_context(tc.manual_schedule())
 
         v_col = const.tile([P, DIN // P], BF16)
-        nc.scalar.dma_start(out=v_col[:], in_=v_last.rearrange("(p c) -> p c", p=P))
+        nc.sync.dma_start(out=v_col[:], in_=v_last.rearrange("(p c) -> p c", p=P))
         v_row = const.tile([P, DIN], BF16)
         nc.vector.memset(v_row[:].bitcast(I32), 0)
-        nc.scalar.dma_start(out=v_row[0:1, :], in_=v_last.rearrange("(o k) -> o k", o=1))
-        ones_f32 = const.tile([P, P], F32)
-        nc.vector.memset(ones_f32[:], 1.0)
-        warm = const.tile([P, 1], F32)
-        nc.scalar.activation(out=warm[:], in_=ones_f32[:, 0:1], func=ACT.Square)
-        d_row = const.tile([P, DOUT], BF16)
-        nc.vector.memset(d_row[:].bitcast(I32), 0)
-        nc.scalar.dma_start(out=d_row[0:1, :], in_=d.rearrange("(o j) -> o j", o=1))
-        bias_row = const.tile([P, DOUT], BF16)
-        nc.vector.memset(bias_row[:].bitcast(I32), 0)
-        nc.scalar.dma_start(out=bias_row[0:1, :], in_=bias.rearrange("(o j) -> o j", o=1))
+        nc.sync.dma_start(out=v_row[0:1, :], in_=v_last.rearrange("(o k) -> o k", o=1))
         u_rows = []
         for a in range(U_CHUNKS):
             rows = rows_pool.tile([P, 2, DIN], BF16, tag="rows")
@@ -63,6 +53,12 @@ def tile_orthogonaldense_pb_kernel(tc, x, u_prev, v_last, d, bias, out):
                 in_=u_prev[a * CHUNK : (a + 1) * CHUNK, :].rearrange("(p r) k -> p r k", r=2),
             )
             u_rows.append(rows)
+        d_row = const.tile([P, DOUT], BF16)
+        nc.vector.memset(d_row[:].bitcast(I32), 0)
+        nc.sync.dma_start(out=d_row[0:1, :], in_=d.rearrange("(o j) -> o j", o=1))
+        bias_row = const.tile([P, DOUT], BF16)
+        nc.vector.memset(bias_row[:].bitcast(I32), 0)
+        nc.sync.dma_start(out=bias_row[0:1, :], in_=bias.rearrange("(o j) -> o j", o=1))
         x_rows = []
         for c in range(X_CHUNKS):
             rows = rows_pool.tile([P, 2, DIN], BF16, tag="rows")
@@ -71,6 +67,11 @@ def tile_orthogonaldense_pb_kernel(tc, x, u_prev, v_last, d, bias, out):
                 in_=x[c * CHUNK : (c + 1) * CHUNK, :].rearrange("(p r) k -> p r k", r=2),
             )
             x_rows.append(rows)
+
+        ones_f32 = const.tile([P, P], F32)
+        nc.vector.memset(ones_f32[:], 1.0)
+        warm = const.tile([P, 1], F32)
+        nc.scalar.activation(out=warm[:], in_=ones_f32[:, 0:1], func=ACT.Square)
 
         ones_bf16 = const.tile([P, P], BF16)
         nc.vector.memset(ones_bf16[:], 1.0)
@@ -266,8 +267,8 @@ def tile_orthogonaldense_pb_kernel(tc, x, u_prev, v_last, d, bias, out):
         for c in range(X_CHUNKS):
             for r in range(2):
                 y_bank(0, c, r)
-            if c % 2 == 0:
-                block = BLOCKS_PER_SWEEP + c // 2
+            block = BLOCKS_PER_SWEEP + c
+            if block < BLOCKS:
                 w_grouped = w_products(block)
                 quantise_w(block, w_grouped)
 

@@ -227,7 +227,7 @@ def tile_orthogonaldense_pb_kernel(tc, x, u_prev, v_last, d, bias, out):
                     stop=(g == PASSES - 1),
                 )
             y_sb = y_pool.tile([P, N_WIDE], F32)
-            if (2 * c + r) % 3 == 1:
+            if sweep == 0 and BLOCKS_PER_SWEEP + c < BLOCKS and r == 1:
                 nc.scalar.copy(out=y_sb[:], in_=bank[:])
                 nc.gpsimd.tensor_tensor(out=y_sb[:], in0=y_sb[:], in1=bias_bc[:, cols], op=ALU.add)
             else:

@@ -38,7 +38,6 @@ def tile_orthogonaldense_pb_kernel(tc, x, u_prev, v_last, d, bias, out):
         keep = stack.enter_context(tc.tile_pool(name="keep", bufs=1))
         y_pool = stack.enter_context(tc.tile_pool(name="y", bufs=8))
         psum = stack.enter_context(tc.psum_pool(name="psum", bufs=8))
-        stack.enter_context(tc.manual_schedule())
 
         v_col = const.tile([P, DIN // P], BF16)
         nc.sync.dma_start(out=v_col[:], in_=v_last.rearrange("(p c) -> p c", p=P))

@@ -32,18 +32,25 @@ assert U_CHUNKS == BLOCKS_PER_SWEEP and X_CHUNKS == 2 * BLOCKS_PER_SWEEP
 def tile_orthogonaldense_pb_kernel(tc, x, u_prev, v_last, d, bias, out):
     nc = tc.nc
     with ExitStack() as stack:
+        stack.enter_context(tc.manual_schedule())
         const = stack.enter_context(tc.tile_pool(name="const", bufs=1))
         rows_pool = stack.enter_context(tc.tile_pool(name="rows", bufs=U_CHUNKS + X_CHUNKS))
         stage = stack.enter_context(tc.tile_pool(name="stage", bufs=4))
         keep = stack.enter_context(tc.tile_pool(name="keep", bufs=1))
-        y_pool = stack.enter_context(tc.tile_pool(name="y", bufs=8))
+        y_pool = stack.enter_context(tc.tile_pool(name="y", bufs=12))
         psum = stack.enter_context(tc.psum_pool(name="psum", bufs=8))
 
         v_col = const.tile([P, DIN // P], BF16)
         nc.sync.dma_start(out=v_col[:], in_=v_last.rearrange("(p c) -> p c", p=P))
         v_row = const.tile([P, DIN], BF16)
         nc.vector.memset(v_row[:].bitcast(I32), 0)
-        nc.sync.dma_start(out=v_row[0:1, :], in_=v_last.rearrange("(o k) -> o k", o=1))
+        nc.scalar.dma_start(out=v_row[0:1, :], in_=v_last.rearrange("(o k) -> o k", o=1))
+        d_row = const.tile([P, DOUT], BF16)
+        nc.vector.memset(d_row[:].bitcast(I32), 0)
+        nc.scalar.dma_start(out=d_row[0:1, :], in_=d.rearrange("(o j) -> o j", o=1))
+        bias_row = const.tile([P, DOUT], BF16)
+        nc.vector.memset(bias_row[:].bitcast(I32), 0)
+        nc.scalar.dma_start(out=bias_row[0:1, :], in_=bias.rearrange("(o j) -> o j", o=1))
         u_rows = []
         for a in range(U_CHUNKS):
             rows = rows_pool.tile([P, 2, DIN], BF16, tag="rows")
@@ -52,12 +59,6 @@ def tile_orthogonaldense_pb_kernel(tc, x, u_prev, v_last, d, bias, out):
                 in_=u_prev[a * CHUNK : (a + 1) * CHUNK, :].rearrange("(p r) k -> p r k", r=2),
             )
             u_rows.append(rows)
-        d_row = const.tile([P, DOUT], BF16)
-        nc.vector.memset(d_row[:].bitcast(I32), 0)
-        nc.sync.dma_start(out=d_row[0:1, :], in_=d.rearrange("(o j) -> o j", o=1))
-        bias_row = const.tile([P, DOUT], BF16)
-        nc.vector.memset(bias_row[:].bitcast(I32), 0)
-        nc.sync.dma_start(out=bias_row[0:1, :], in_=bias.rearrange("(o j) -> o j", o=1))
         x_rows = []
         for c in range(X_CHUNKS):
             rows = rows_pool.tile([P, 2, DIN], BF16, tag="rows")
@@ -176,42 +177,49 @@ def tile_orthogonaldense_pb_kernel(tc, x, u_prev, v_last, d, bias, out):
                 in_=h_grouped[:].rearrange("p g j t -> p (g j t)"),
             )
 
-        def w_products(block):
-            cols = slice(block * P, (block + 1) * P)
-            w_grouped = stage.tile([P, PASSES, P, PACK], BF16, align_bytes=64)
-            for gi in range(PASSES):
-                bank = psum.tile([P, PACK, P], F32, tag="bank")
-                for t in range(PACK):
-                    chunk = 2 * gi + t // 2
-                    rows_e = slice((t % 2) * P, (t % 2 + 1) * P)
-                    for g in range(PASSES):
-                        nc.tensor.matmul_mx(
-                            out=bank[:, t, :],
-                            lhsT=u_codes[:, chunk, g, rows_e].bitcast(FP8X4),
-                            lhsT_scale=u_scales[:, chunk, g, rows_e],
-                            rhs=h_codes[:, block, g, :].bitcast(FP8X4),
-                            rhs_scale=h_scales[:, block, g, :],
-                            start=(g == 0),
-                            stop=(g == PASSES - 1),
-                        )
-                nc.vector.tensor_tensor(
-                    out=w_grouped[:, gi],
-                    in0=bank[:].rearrange("p t j -> p j t"),
-                    in1=d_bc[:, cols].unsqueeze(2).to_broadcast([P, P, PACK]),
-                    op=ALU.mult,
-                )
-            return w_grouped
+        w_halves = {}
 
-        def quantise_w(block, w_grouped):
+        def w_products(block, gi):
             cols = slice(block * P, (block + 1) * P)
-            for gi in range(PASSES):
-                nc.vector.quantize_mx(
-                    out=w_codes[:, gi, cols].bitcast(FP8X4),
-                    scales=w_scales[:, gi, cols],
-                    in_=w_grouped[:, gi].rearrange("p j t -> p (j t)"),
-                )
+            w_grouped = stage.tile([P, P, PACK], BF16, align_bytes=64)
+            bank = psum.tile([P, PACK, P], F32, tag="bank")
+            for t in range(PACK):
+                chunk = 2 * gi + t // 2
+                rows_e = slice((t % 2) * P, (t % 2 + 1) * P)
+                for g in range(PASSES):
+                    nc.tensor.matmul_mx(
+                        out=bank[:, t, :],
+                        lhsT=u_codes[:, chunk, g, rows_e].bitcast(FP8X4),
+                        lhsT_scale=u_scales[:, chunk, g, rows_e],
+                        rhs=h_codes[:, block, g, :].bitcast(FP8X4),
+                        rhs_scale=h_scales[:, block, g, :],
+                        start=(g == 0),
+                        stop=(g == PASSES - 1),
+                    )
+            nc.vector.tensor_tensor(
+                out=w_grouped[:],
+                in0=bank[:].rearrange("p t j -> p j t"),
+                in1=d_bc[:, cols].unsqueeze(2).to_broadcast([P, P, PACK]),
+                op=ALU.mult,
+            )
+            w_halves[block, gi] = w_grouped
 
-        def y_bank(sweep, c, r):
+        def quantise_w(block, gi):
+            cols = slice(block * P, (block + 1) * P)
+            nc.vector.quantize_mx(
+                out=w_codes[:, gi, cols].bitcast(FP8X4),
+                scales=w_scales[:, gi, cols],
+                in_=w_halves[block, gi][:].rearrange("p j t -> p (j t)"),
+            )
+
+        late_stores = []
+
+        def store(sweep, c, r, y_sb):
+            cols = slice(sweep * N_WIDE, (sweep + 1) * N_WIDE)
+            y_rows = out[c * CHUNK : (c + 1) * CHUNK, :].rearrange("(p r) j -> p r j", r=2)
+            nc.sync.dma_start(out=y_rows[:, r, cols], in_=y_sb[:])
+
+        def y_bank(sweep, c, r, through_scalar):
             cols = slice(sweep * N_WIDE, (sweep + 1) * N_WIDE)
             rows_r = slice(r * P, (r + 1) * P)
             bank = psum.tile([P, N_WIDE], F32, tag="bank")
@@ -226,51 +234,111 @@ def tile_orthogonaldense_pb_kernel(tc, x, u_prev, v_last, d, bias, out):
                     stop=(g == PASSES - 1),
                 )
             y_sb = y_pool.tile([P, N_WIDE], F32)
-            if sweep == 0 and BLOCKS_PER_SWEEP + c < BLOCKS and r == 1:
+            if through_scalar:
                 nc.scalar.copy(out=y_sb[:], in_=bank[:])
                 nc.gpsimd.tensor_tensor(out=y_sb[:], in0=y_sb[:], in1=bias_bc[:, cols], op=ALU.add)
+                late_stores.append([3, (sweep, c, r, y_sb)])
             else:
                 nc.vector.tensor_tensor(out=y_sb[:], in0=bank[:], in1=bias_bc[:, cols], op=ALU.add)
-            y_rows = out[c * CHUNK : (c + 1) * CHUNK, :].rearrange("(p r) j -> p r j", r=2)
-            nc.sync.dma_start(out=y_rows[:, r, cols], in_=y_sb[:])
+                store(sweep, c, r, y_sb)
+            for late in list(late_stores):
+                late[0] = late[0] - 1
+                if late[0] == 0:
+                    store(*late[1])
+                    late_stores.remove(late)
 
+        h_blocks = {}
+        grouped_rows = {}
 
-        reflection_factor()
-        h_grouped = []
-        u_grouped = []
-        for a in range(U_CHUNKS):
-            h_grouped.append(h_products(a))
-            u_grouped.append(transpose_rows(u_rows[a]))
-            if a > 0:
-                quantise_h(a - 1, h_grouped[a - 1])
-                quantise_rows(u_grouped[a - 1], u_codes[:, a - 1], u_scales[:, a - 1])
-        last = U_CHUNKS - 1
-        quantise_h(last, h_grouped[last])
+        def make_h(block):
+            h_blocks[block] = h_products(block)
+
+        def finish_h(block):
+            quantise_h(block, h_blocks[block])
+
+        def turn(kind, c):
+            grouped_rows[kind, c] = transpose_rows((u_rows if kind == "u" else x_rows)[c])
+
+        def finish_u(c):
+            quantise_rows(grouped_rows["u", c], u_codes[:, c], u_scales[:, c])
+
+        def finish_x(c):
+            quantise_rows(grouped_rows["x", c], x_codes[:, c], x_scales[:, c])
+
         d_bc = const.tile([P, DOUT], BF16)
-        spread(d_row, d_bc)
-        quantise_rows(u_grouped[last], u_codes[:, last], u_scales[:, last])
         bias_bc = const.tile([P, DOUT], BF16)
+        spread(d_row, d_bc)
+        reflection_factor()
+        make_h(0)
+        turn("u", 0)
+        make_h(1)
+        turn("u", 1)
+        finish_h(0)
         spread(bias_row, bias_bc)
+        finish_u(0)
+        make_h(2)
+        finish_h(1)
+        turn("u", 2)
+        finish_u(1)
+        make_h(3)
+        finish_h(2)
+        w_products(0, 0)
+        turn("u", 3)
+        finish_u(2)
+        finish_h(3)
+        w_products(1, 0)
+        quantise_w(0, 0)
+        finish_u(3)
+        turn("x", 0)
+        w_products(2, 0)
+        quantise_w(1, 0)
+        w_products(3, 0)
+        quantise_w(2, 0)
+        w_products(0, 1)
+        quantise_w(3, 0)
+        turn("x", 1)
+        w_products(1, 1)
+        quantise_w(0, 1)
+        w_products(2, 1)
+        quantise_w(1, 1)
+        finish_x(0)
+        make_h(4)
+        w_products(3, 1)
+        quantise_w(2, 1)
+        quantise_w(3, 1)
+        turn("x", 2)
+        finish_h(4)
+        finish_x(1)
+        make_h(5)
 
-        for block in range(BLOCKS_PER_SWEEP):
-            later = block + BLOCKS_PER_SWEEP
-            h_later = h_products(later)
-            w_grouped = w_products(block)
-            x_grouped = [transpose_rows(x_rows[2 * block + i]) for i in range(2)]
-            quantise_w(block, w_grouped)
-            quantise_h(later, h_later)
-            for i in range(2):
-                c = 2 * block + i
-                quantise_rows(x_grouped[i], x_codes[:, c], x_scales[:, c])
+        for c in range(4):
+            later = 4 + c
+            y_bank(0, c, 0, False)
+            w_products(later, 0)
+            if c < 3:
+                finish_h(later + 1)
+            y_bank(0, c, 1, True)
+            w_products(later, 1)
+            quantise_w(later, 0)
+            if c < 2:
+                make_h(later + 2)
+            finish_x(c + 2)
+            turn("x", c + 3)
+            quantise_w(later, 1)
 
-        for c in range(X_CHUNKS):
+        y_bank(0, 4, 0, False)
+        y_bank(0, 4, 1, True)
+        finish_x(6)
+        y_bank(0, 5, 0, False)
+        turn("x", 7)
+        y_bank(0, 5, 1, True)
+        y_bank(1, 0, 0, False)
+        finish_x(7)
+        y_bank(1, 0, 1, False)
+        for c in (6, 7):
+            for sweep, chunk in ((0, c), (1, c - 5)):
+                for r in range(2):
+                    y_bank(sweep, chunk, r, sweep == 0 and r == 1)
+        for c in range(3, 8):
             for r in range(2):
-                y_bank(0, c, r)
-            block = BLOCKS_PER_SWEEP + c
-            if block < BLOCKS:
-                w_grouped = w_products(block)
-                quantise_w(block, w_grouped)
-
-        for c in range(X_CHUNKS):
-            for r in range(2):
-                y_bank(1, c, r)
+                y_bank(1, c, r, False)

@@ -43,14 +43,11 @@ def tile_orthogonaldense_pb_kernel(tc, x, u_prev, v_last, d, bias, out):
         v_col = const.tile([P, DIN // P], BF16)
         nc.sync.dma_start(out=v_col[:], in_=v_last.rearrange("(p c) -> p c", p=P))
         v_row = const.tile([P, DIN], BF16)
-        nc.vector.memset(v_row[:].bitcast(I32), 0)
-        nc.scalar.dma_start(out=v_row[0:1, :], in_=v_last.rearrange("(o k) -> o k", o=1))
+        nc.gpsimd.memset(v_row[:].bitcast(I32), 0)
+        nc.sync.dma_start(out=v_row[0:1, :], in_=v_last.rearrange("(o k) -> o k", o=1))
         d_row = const.tile([P, DOUT], BF16)
         nc.vector.memset(d_row[:].bitcast(I32), 0)
-        nc.scalar.dma_start(out=d_row[0:1, :], in_=d.rearrange("(o j) -> o j", o=1))
-        bias_row = const.tile([P, DOUT], BF16)
-        nc.vector.memset(bias_row[:].bitcast(I32), 0)
-        nc.scalar.dma_start(out=bias_row[0:1, :], in_=bias.rearrange("(o j) -> o j", o=1))
+        nc.sync.dma_start(out=d_row[0:1, :], in_=d.rearrange("(o j) -> o j", o=1))
         u_rows = []
         for a in range(U_CHUNKS):
             rows = rows_pool.tile([P, 2, DIN], BF16, tag="rows")
@@ -67,6 +64,8 @@ def tile_orthogonaldense_pb_kernel(tc, x, u_prev, v_last, d, bias, out):
                 in_=x[c * CHUNK : (c + 1) * CHUNK, :].rearrange("(p r) k -> p r k", r=2),
             )
             x_rows.append(rows)
+        bias_bc = const.tile([P, DOUT], BF16)
+        nc.sync.dma_start(out=bias_bc[:], in_=bias.partition_broadcast(P))
 
         ones_f32 = const.tile([P, P], F32)
         nc.vector.memset(ones_f32[:], 1.0)
@@ -214,12 +213,7 @@ def tile_orthogonaldense_pb_kernel(tc, x, u_prev, v_last, d, bias, out):
 
         late_stores = []
 
-        def store(sweep, c, r, y_sb):
-            cols = slice(sweep * N_WIDE, (sweep + 1) * N_WIDE)
-            y_rows = out[c * CHUNK : (c + 1) * CHUNK, :].rearrange("(p r) j -> p r j", r=2)
-            nc.sync.dma_start(out=y_rows[:, r, cols], in_=y_sb[:])
-
-        def y_bank(sweep, c, r, through_scalar):
+        def y_product(sweep, c, r):
             cols = slice(sweep * N_WIDE, (sweep + 1) * N_WIDE)
             rows_r = slice(r * P, (r + 1) * P)
             bank = psum.tile([P, N_WIDE], F32, tag="bank")
@@ -233,19 +227,46 @@ def tile_orthogonaldense_pb_kernel(tc, x, u_prev, v_last, d, bias, out):
                     start=(g == 0),
                     stop=(g == PASSES - 1),
                 )
+            return bank
+
+        def y_rows(c, r):
+            return out[c * CHUNK : (c + 1) * CHUNK, :].rearrange("(p r) j -> p r j", r=2)[:, r]
+
+        def y_half(sweep, c, r, through_scalar=False):
+            cols = slice(sweep * N_WIDE, (sweep + 1) * N_WIDE)
+            bank = y_product(sweep, c, r)
             y_sb = y_pool.tile([P, N_WIDE], F32)
             if through_scalar:
                 nc.scalar.copy(out=y_sb[:], in_=bank[:])
                 nc.gpsimd.tensor_tensor(out=y_sb[:], in0=y_sb[:], in1=bias_bc[:, cols], op=ALU.add)
-                late_stores.append([3, (sweep, c, r, y_sb)])
+                late_stores.append([3, (y_rows(c, r)[:, cols], y_sb)])
             else:
                 nc.vector.tensor_tensor(out=y_sb[:], in0=bank[:], in1=bias_bc[:, cols], op=ALU.add)
-                store(sweep, c, r, y_sb)
+                nc.sync.dma_start(out=y_rows(c, r)[:, cols], in_=y_sb[:])
+            issue_late()
+
+        def issue_late():
             for late in list(late_stores):
                 late[0] = late[0] - 1
                 if late[0] == 0:
-                    store(*late[1])
+                    nc.sync.dma_start(out=late[1][0], in_=late[1][1][:])
                     late_stores.remove(late)
+
+        whole_rows = {}
+
+        def y_part(sweep, c, r):
+            cols = slice(sweep * N_WIDE, (sweep + 1) * N_WIDE)
+            bank = y_product(sweep, c, r)
+            if sweep == 0:
+                y_whole = y_pool.tile([P, DOUT], F32, bufs=6)
+                whole_rows[c, r] = y_whole
+            y_whole = whole_rows[c, r]
+            nc.vector.tensor_tensor(
+                out=y_whole[:, cols], in0=bank[:], in1=bias_bc[:, cols], op=ALU.add
+            )
+            if sweep == 1:
+                nc.sync.dma_start(out=y_rows(c, r), in_=y_whole[:])
+            issue_late()
 
         h_blocks = {}
         grouped_rows = {}
@@ -266,17 +287,15 @@ def tile_orthogonaldense_pb_kernel(tc, x, u_prev, v_last, d, bias, out):
             quantise_rows(grouped_rows["x", c], x_codes[:, c], x_scales[:, c])
 
         d_bc = const.tile([P, DOUT], BF16)
-        bias_bc = const.tile([P, DOUT], BF16)
-        spread(d_row, d_bc)
         reflection_factor()
+        spread(d_row, d_bc)
         make_h(0)
         turn("u", 0)
         make_h(1)
         turn("u", 1)
         finish_h(0)
-        spread(bias_row, bias_bc)
-        finish_u(0)
         make_h(2)
+        finish_u(0)
         finish_h(1)
         turn("u", 2)
         finish_u(1)
@@ -285,9 +304,9 @@ def tile_orthogonaldense_pb_kernel(tc, x, u_prev, v_last, d, bias, out):
         w_products(0, 0)
         turn("u", 3)
         finish_u(2)
-        finish_h(3)
         w_products(1, 0)
         quantise_w(0, 0)
+        finish_h(3)
         finish_u(3)
         turn("x", 0)
         w_products(2, 0)
@@ -302,10 +321,10 @@ def tile_orthogonaldense_pb_kernel(tc, x, u_prev, v_last, d, bias, out):
         w_products(2, 1)
         quantise_w(1, 1)
         finish_x(0)
-        make_h(4)
         w_products(3, 1)
         quantise_w(2, 1)
         quantise_w(3, 1)
+        make_h(4)
         turn("x", 2)
         finish_h(4)
         finish_x(1)
@@ -313,32 +332,46 @@ def tile_orthogonaldense_pb_kernel(tc, x, u_prev, v_last, d, bias, out):
 
         for c in range(4):
             later = 4 + c
-            y_bank(0, c, 0, False)
+            y_half(0, c, 0)
             w_products(later, 0)
             if c < 3:
                 finish_h(later + 1)
-            y_bank(0, c, 1, True)
+                finish_x(c + 2)
+            y_half(0, c, 1, True)
+            if c < 3:
+                turn("x", c + 3)
             w_products(later, 1)
             quantise_w(later, 0)
             if c < 2:
                 make_h(later + 2)
-            finish_x(c + 2)
-            turn("x", c + 3)
             quantise_w(later, 1)
 
-        y_bank(0, 4, 0, False)
-        y_bank(0, 4, 1, True)
+        y_part(0, 4, 0)
+        finish_x(5)
+        y_part(0, 4, 1)
+        turn("x", 6)
+        y_part(1, 4, 0)
+        y_part(1, 4, 1)
+        y_part(0, 5, 0)
         finish_x(6)
-        y_bank(0, 5, 0, False)
+        y_part(1, 5, 0)
         turn("x", 7)
-        y_bank(0, 5, 1, True)
-        y_bank(1, 0, 0, False)
+        y_part(0, 5, 1)
+        y_part(1, 5, 1)
+        y_half(1, 0, 0)
+        y_half(1, 0, 1, True)
         finish_x(7)
-        y_bank(1, 0, 1, False)
-        for c in (6, 7):
-            for sweep, chunk in ((0, c), (1, c - 5)):
-                for r in range(2):
-                    y_bank(sweep, chunk, r, sweep == 0 and r == 1)
-        for c in range(3, 8):
-            for r in range(2):
-                y_bank(1, c, r, False)
+        y_part(0, 6, 0)
+        y_part(1, 6, 0)
+        y_half(1, 1, 0)
+        y_half(1, 1, 1, True)
+        y_part(0, 6, 1)
+        y_part(1, 6, 1)
+        y_half(1, 2, 0)
+        y_half(1, 2, 1)
+        y_part(0, 7, 0)
+        y_part(1, 7, 0)
+        y_half(1, 3, 0)
+        y_half(1, 3, 1)
+        y_half(0, 7, 1)
+        y_half(1, 7, 1)

@@ -64,8 +64,9 @@ def tile_orthogonaldense_pb_kernel(tc, x, u_prev, v_last, d, bias, out):
                 in_=x[c * CHUNK : (c + 1) * CHUNK, :].rearrange("(p r) k -> p r k", r=2),
             )
             x_rows.append(rows)
-        bias_bc = const.tile([P, DOUT], BF16)
-        nc.sync.dma_start(out=bias_bc[:], in_=bias.partition_broadcast(P))
+            if c == 2:
+                bias_bc = const.tile([P, DOUT], BF16)
+                nc.sync.dma_start(out=bias_bc[:], in_=bias.partition_broadcast(P))
 
         ones_f32 = const.tile([P, P], F32)
         nc.vector.memset(ones_f32[:], 1.0)
@@ -332,46 +333,52 @@ def tile_orthogonaldense_pb_kernel(tc, x, u_prev, v_last, d, bias, out):
 
         for c in range(4):
             later = 4 + c
-            y_half(0, c, 0)
+            y_half(0, c, 0, True)
             w_products(later, 0)
             if c < 3:
                 finish_h(later + 1)
+            if c < 2:
                 finish_x(c + 2)
+            if c == 3:
+                finish_x(4)
             y_half(0, c, 1, True)
-            if c < 3:
-                turn("x", c + 3)
+            if c == 0:
+                turn("x", 3)
+            if c == 2:
+                turn("x", 4)
             w_products(later, 1)
             quantise_w(later, 0)
             if c < 2:
                 make_h(later + 2)
             quantise_w(later, 1)
 
+        turn("x", 5)
         y_part(0, 4, 0)
-        finish_x(5)
         y_part(0, 4, 1)
-        turn("x", 6)
         y_part(1, 4, 0)
+        finish_x(5)
         y_part(1, 4, 1)
+        y_half(1, 0, 0, False)
+        y_half(1, 0, 1, True)
+        turn("x", 6)
         y_part(0, 5, 0)
-        finish_x(6)
         y_part(1, 5, 0)
-        turn("x", 7)
+        finish_x(6)
         y_part(0, 5, 1)
         y_part(1, 5, 1)
-        y_half(1, 0, 0)
-        y_half(1, 0, 1, True)
-        finish_x(7)
+        y_half(1, 1, 0, True)
+        y_half(1, 1, 1, True)
+        turn("x", 7)
         y_part(0, 6, 0)
         y_part(1, 6, 0)
-        y_half(1, 1, 0)
-        y_half(1, 1, 1, True)
         y_part(0, 6, 1)
+        finish_x(7)
         y_part(1, 6, 1)
-        y_half(1, 2, 0)
-        y_half(1, 2, 1)
+        y_half(1, 2, 0, True)
+        y_half(1, 2, 1, False)
+        y_half(1, 3, 0, False)
+        y_half(1, 3, 1, False)
         y_part(0, 7, 0)
         y_part(1, 7, 0)
-        y_half(1, 3, 0)
-        y_half(1, 3, 1)
-        y_half(0, 7, 1)
-        y_half(1, 7, 1)
+        y_part(0, 7, 1)
+        y_part(1, 7, 1)

@@ -68,10 +68,10 @@ def tile_orthogonaldense_pb_kernel(tc, x, u_prev, v_last, d, bias, out):
                 bias_bc = const.tile([P, DOUT], BF16)
                 nc.sync.dma_start(out=bias_bc[:], in_=bias.partition_broadcast(P))
 
-        ones_f32 = const.tile([P, P], F32)
-        nc.vector.memset(ones_f32[:], 1.0)
+        minus_half = const.tile([P, P], F32)
+        nc.vector.memset(minus_half[:], -0.5)
         warm = const.tile([P, 1], F32)
-        nc.scalar.activation(out=warm[:], in_=ones_f32[:, 0:1], func=ACT.Square)
+        nc.scalar.activation(out=warm[:], in_=minus_half[:, 0:1], func=ACT.Square)
 
         ones_bf16 = const.tile([P, P], BF16)
         nc.vector.memset(ones_bf16[:], 1.0)
@@ -83,6 +83,11 @@ def tile_orthogonaldense_pb_kernel(tc, x, u_prev, v_last, d, bias, out):
             for e in range(2):
                 nc.vector.tensor_copy(out=eye[:, u, :, e, 2 * u + e], in_=ident[:])
         eye_cols = eye[:].rearrange("p u q e t -> p (u q e) t")
+        spot = const.tile([P, 2, CHUNK], BF16)
+        nc.gpsimd.memset(spot[:].rearrange("p e c -> p (e c)").bitcast(I32), 0)
+        spot_split = spot[:].rearrange("p e (q x) -> p e q x", x=2)
+        for e in range(2):
+            nc.gpsimd.tensor_copy(out=spot_split[:, e, :, e], in_=ident[:])
 
         u_codes = keep.tile([P, U_CHUNKS, PASSES, CHUNK], U32, align_bytes=64)
         u_scales = keep.tile([P, U_CHUNKS, PASSES, CHUNK], U8, align_bytes=64)
@@ -118,25 +123,35 @@ def tile_orthogonaldense_pb_kernel(tc, x, u_prev, v_last, d, bias, out):
             )
 
         factor = const.tile([P, 1], F32)
+        diagonal = const.tile([P, P], F32)
+        diagonal_high = const.tile([P, P], BF16)
+        diagonal_low = const.tile([P, P], BF16)
 
         def reflection_factor():
             squares = const.tile([P, DIN // P], F32)
             partial = const.tile([P, 1], F32)
             nc.scalar.activation(out=squares[:], in_=v_col[:], func=ACT.Square, accum_out=partial[:])
             total = psum.tile([P, 1], F32, tag="bank")
-            nc.tensor.matmul(out=total[:], lhsT=ones_f32[:], rhs=partial[:], start=True, stop=True)
-            denominator = const.tile([P, 1], F32)
-            nc.vector.tensor_scalar_mul(out=denominator[:], in0=total[:], scalar1=-0.5)
-            nc.vector.reciprocal(out=factor[:], in_=denominator[:])
+            nc.tensor.matmul(out=total[:], lhsT=minus_half[:], rhs=partial[:], start=True, stop=True)
+            nc.vector.reciprocal(out=factor[:], in_=total[:])
+            inverse = const.tile([P, 1], F32)
+            nc.scalar.copy(out=inverse[:], in_=total[:])
+            nc.gpsimd.tensor_scalar(
+                out=diagonal[:], in0=ident[:], scalar1=inverse[:, 0:1], scalar2=None, op0=ALU.mult
+            )
+            nc.gpsimd.tensor_copy(out=diagonal_high[:], in_=diagonal[:])
+            nc.gpsimd.tensor_tensor(
+                out=diagonal_low[:], in0=diagonal[:], in1=diagonal_high[:], op=ALU.subtract
+            )
 
-        def spread(row, everywhere):
+        def spread(row):
             bank = psum.tile([P, DOUT], BF16, tag="bank")
             for half in range(DOUT // N_WIDE):
                 cols = slice(half * N_WIDE, (half + 1) * N_WIDE)
                 nc.tensor.matmul(
                     out=bank[:, cols], lhsT=ones_bf16[:], rhs=row[:, cols], start=True, stop=True
                 )
-            nc.scalar.copy(out=everywhere[:], in_=bank[:])
+            return bank
 
         v_by_word = v_row[:].rearrange("p (g u m e) -> p g u e m", g=PASSES, u=2, e=2)
 
@@ -146,15 +161,24 @@ def tile_orthogonaldense_pb_kernel(tc, x, u_prev, v_last, d, bias, out):
             for g in range(PASSES):
                 bank = psum.tile([P, PACK, P], F32, tag="bank")
                 for t in range(PACK):
+                    add_here = block >= BLOCKS_PER_SWEEP and 2 * g + t // 2 == block // 2
                     nc.tensor.matmul(
                         out=bank[:, t, :],
                         lhsT=v_by_word[:, g, t // 2, t % 2, :],
                         rhs=v_row[:, cols],
                         start=True,
-                        stop=True,
+                        stop=not add_here,
                     )
+                    if add_here:
+                        place = spot[:, t % 2, (block % 2) * P : (block % 2 + 1) * P]
+                        nc.tensor.matmul(
+                            out=bank[:, t, :], lhsT=diagonal_high[:], rhs=place, start=False, stop=False
+                        )
+                        nc.tensor.matmul(
+                            out=bank[:, t, :], lhsT=diagonal_low[:], rhs=place, start=False, stop=True
+                        )
                 products = bank[:].rearrange("p t j -> p j t")
-                if g == block // BLOCKS_PER_SWEEP:
+                if block < BLOCKS_PER_SWEEP and g == 0:
                     first = (block % BLOCKS_PER_SWEEP) * P
                     nc.vector.scalar_tensor_tensor(
                         out=h_grouped[:, g],
@@ -181,7 +205,9 @@ def tile_orthogonaldense_pb_kernel(tc, x, u_prev, v_last, d, bias, out):
 
         def w_products(block, gi):
             cols = slice(block * P, (block + 1) * P)
-            w_grouped = stage.tile([P, P, PACK], BF16, align_bytes=64)
+            if block % 2 == 0:
+                w_pair = stage.tile([P, 2, P, PACK], BF16, align_bytes=64)
+                w_halves[block // 2, gi] = w_pair
             bank = psum.tile([P, PACK, P], F32, tag="bank")
             for t in range(PACK):
                 chunk = 2 * gi + t // 2
@@ -197,19 +223,18 @@ def tile_orthogonaldense_pb_kernel(tc, x, u_prev, v_last, d, bias, out):
                         stop=(g == PASSES - 1),
                     )
             nc.vector.tensor_tensor(
-                out=w_grouped[:],
+                out=w_halves[block // 2, gi][:, block % 2],
                 in0=bank[:].rearrange("p t j -> p j t"),
                 in1=d_bc[:, cols].unsqueeze(2).to_broadcast([P, P, PACK]),
                 op=ALU.mult,
             )
-            w_halves[block, gi] = w_grouped
 
-        def quantise_w(block, gi):
-            cols = slice(block * P, (block + 1) * P)
+        def quantise_w(pair, gi):
+            cols = slice(pair * 2 * P, (pair + 1) * 2 * P)
             nc.vector.quantize_mx(
                 out=w_codes[:, gi, cols].bitcast(FP8X4),
                 scales=w_scales[:, gi, cols],
-                in_=w_halves[block, gi][:].rearrange("p j t -> p (j t)"),
+                in_=w_halves[pair, gi][:].rearrange("p b j t -> p (b j t)"),
             )
 
         late_stores = []
@@ -239,7 +264,12 @@ def tile_orthogonaldense_pb_kernel(tc, x, u_prev, v_last, d, bias, out):
             y_sb = y_pool.tile([P, N_WIDE], F32)
             if through_scalar:
                 nc.scalar.copy(out=y_sb[:], in_=bank[:])
-                nc.gpsimd.tensor_tensor(out=y_sb[:], in0=y_sb[:], in1=bias_bc[:, cols], op=ALU.add)
+                for part in range(2):
+                    some = slice(part * N_WIDE // 2, (part + 1) * N_WIDE // 2)
+                    biases = bias_bc[:, cols][:, some]
+                    nc.gpsimd.tensor_tensor(
+                        out=y_sb[:, some], in0=y_sb[:, some], in1=biases, op=ALU.add
+                    )
                 late_stores.append([3, (y_rows(c, r)[:, cols], y_sb)])
             else:
                 nc.vector.tensor_tensor(out=y_sb[:], in0=bank[:], in1=bias_bc[:, cols], op=ALU.add)
@@ -289,43 +319,40 @@ def tile_orthogonaldense_pb_kernel(tc, x, u_prev, v_last, d, bias, out):
 
         d_bc = const.tile([P, DOUT], BF16)
         reflection_factor()
-        spread(d_row, d_bc)
         make_h(0)
-        turn("u", 0)
         make_h(1)
-        turn("u", 1)
         finish_h(0)
+        finish_h(1)
+        turn("u", 0)
         make_h(2)
         finish_u(0)
-        finish_h(1)
-        turn("u", 2)
-        finish_u(1)
+        turn("u", 1)
         make_h(3)
         finish_h(2)
-        w_products(0, 0)
+        d_bank = spread(d_row)
+        turn("u", 2)
+        finish_u(1)
         turn("u", 3)
+        finish_h(3)
+        nc.vector.tensor_copy(out=d_bc[:], in_=d_bank[:])
+        w_products(0, 0)
         finish_u(2)
         w_products(1, 0)
-        quantise_w(0, 0)
-        finish_h(3)
         finish_u(3)
-        turn("x", 0)
         w_products(2, 0)
-        quantise_w(1, 0)
+        quantise_w(0, 0)
+        turn("x", 0)
         w_products(3, 0)
-        quantise_w(2, 0)
         w_products(0, 1)
-        quantise_w(3, 0)
-        turn("x", 1)
+        quantise_w(1, 0)
         w_products(1, 1)
-        quantise_w(0, 1)
+        turn("x", 1)
         w_products(2, 1)
-        quantise_w(1, 1)
-        finish_x(0)
+        quantise_w(0, 1)
         w_products(3, 1)
-        quantise_w(2, 1)
-        quantise_w(3, 1)
+        finish_x(0)
         make_h(4)
+        quantise_w(1, 1)
         turn("x", 2)
         finish_h(4)
         finish_x(1)
@@ -333,10 +360,12 @@ def tile_orthogonaldense_pb_kernel(tc, x, u_prev, v_last, d, bias, out):
 
         for c in range(4):
             later = 4 + c
-            y_half(0, c, 0, True)
+            y_half(0, c, 0, False)
             w_products(later, 0)
             if c < 3:
                 finish_h(later + 1)
+            if c == 2:
+                quantise_w(2, 1)
             if c < 2:
                 finish_x(c + 2)
             if c == 3:
@@ -347,10 +376,11 @@ def tile_orthogonaldense_pb_kernel(tc, x, u_prev, v_last, d, bias, out):
             if c == 2:
                 turn("x", 4)
             w_products(later, 1)
-            quantise_w(later, 0)
+            if c % 2 == 1:
+                quantise_w(later // 2, 0)
             if c < 2:
                 make_h(later + 2)
-            quantise_w(later, 1)
+        quantise_w(3, 1)
 
         turn("x", 5)
         y_part(0, 4, 0)

@@ -47,7 +47,6 @@ def tile_orthogonaldense_pb_kernel(tc, x, u_prev, v_last, d, bias, out):
         nc.sync.dma_start(out=v_row[0:1, :], in_=v_last.rearrange("(o k) -> o k", o=1))
         d_row = const.tile([P, DOUT], BF16)
         nc.vector.memset(d_row[:].bitcast(I32), 0)
-        nc.sync.dma_start(out=d_row[0:1, :], in_=d.rearrange("(o j) -> o j", o=1))
         u_rows = []
         for a in range(U_CHUNKS):
             rows = rows_pool.tile([P, 2, DIN], BF16, tag="rows")
@@ -56,6 +55,8 @@ def tile_orthogonaldense_pb_kernel(tc, x, u_prev, v_last, d, bias, out):
                 in_=u_prev[a * CHUNK : (a + 1) * CHUNK, :].rearrange("(p r) k -> p r k", r=2),
             )
             u_rows.append(rows)
+            if a == 1:
+                nc.sync.dma_start(out=d_row[0:1, :], in_=d.rearrange("(o j) -> o j", o=1))
         x_rows = []
         for c in range(X_CHUNKS):
             rows = rows_pool.tile([P, 2, DIN], BF16, tag="rows")
@@ -79,15 +80,25 @@ def tile_orthogonaldense_pb_kernel(tc, x, u_prev, v_last, d, bias, out):
         make_identity(nc, ident[:])
         eye = const.tile([P, 2, P, 2, PACK], BF16)
         nc.vector.memset(eye[:].rearrange("p u q e t -> p (u q e t)").bitcast(I32), 0)
+        eye_pairs = eye[:].rearrange("p u q e t -> p u q (e t)")
         for u in range(2):
-            for e in range(2):
-                nc.vector.tensor_copy(out=eye[:, u, :, e, 2 * u + e], in_=ident[:])
+            nc.vector.tensor_copy(
+                out=eye_pairs[:, u, :, 2 * u : 2 * u + 6 : 5],
+                in_=ident[:].unsqueeze(2).to_broadcast([P, P, 2]),
+            )
         eye_cols = eye[:].rearrange("p u q e t -> p (u q e) t")
         spot = const.tile([P, 2, CHUNK], BF16)
         nc.gpsimd.memset(spot[:].rearrange("p e c -> p (e c)").bitcast(I32), 0)
         spot_split = spot[:].rearrange("p e (q x) -> p e q x", x=2)
         for e in range(2):
-            nc.gpsimd.tensor_copy(out=spot_split[:, e, :, e], in_=ident[:])
+            nc.gpsimd.tensor_scalar(
+                out=spot_split[:, e, :, e],
+                in0=ident[:],
+                scalar1=1.0,
+                scalar2=0.0,
+                op0=ALU.mult,
+                op1=ALU.add,
+            )
 
         u_codes = keep.tile([P, U_CHUNKS, PASSES, CHUNK], U32, align_bytes=64)
         u_scales = keep.tile([P, U_CHUNKS, PASSES, CHUNK], U8, align_bytes=64)
@@ -137,9 +148,21 @@ def tile_orthogonaldense_pb_kernel(tc, x, u_prev, v_last, d, bias, out):
             inverse = const.tile([P, 1], F32)
             nc.scalar.copy(out=inverse[:], in_=total[:])
             nc.gpsimd.tensor_scalar(
-                out=diagonal[:], in0=ident[:], scalar1=inverse[:, 0:1], scalar2=None, op0=ALU.mult
+                out=diagonal[:],
+                in0=ident[:],
+                scalar1=inverse[:, 0:1],
+                scalar2=0.0,
+                op0=ALU.mult,
+                op1=ALU.add,
             )
-            nc.gpsimd.tensor_copy(out=diagonal_high[:], in_=diagonal[:])
+            nc.gpsimd.tensor_scalar(
+                out=diagonal_high[:],
+                in0=diagonal[:],
+                scalar1=1.0,
+                scalar2=0.0,
+                op0=ALU.mult,
+                op1=ALU.add,
+            )
             nc.gpsimd.tensor_tensor(
                 out=diagonal_low[:], in0=diagonal[:], in1=diagonal_high[:], op=ALU.subtract
             )

from contextlib import ExitStack

import concourse.mybir as mybir
from concourse.masks import make_identity

FP8X4 = mybir.dt.float8_e4m3fn_x4
BF16 = mybir.dt.bfloat16
F32 = mybir.dt.float32
U32 = mybir.dt.uint32
U8 = mybir.dt.uint8
I32 = mybir.dt.int32
ALU = mybir.AluOpType
ACT = mybir.ActivationFunctionType

B, DIN, DOUT = 2048, 1024, 1024
FLOPS = 2 * DIN * DIN * DOUT + 2 * B * DIN * DOUT

P = 128
PACK = 4
K_PASS = P * PACK
PASSES = DIN // K_PASS
CHUNK = 2 * P
U_CHUNKS = DIN // CHUNK
X_CHUNKS = B // CHUNK
BLOCKS = DOUT // P
N_WIDE = 512
SWEEPS = DOUT // N_WIDE
BLOCKS_PER_SWEEP = BLOCKS // SWEEPS
assert U_CHUNKS == BLOCKS_PER_SWEEP and X_CHUNKS == 2 * BLOCKS_PER_SWEEP


def tile_orthogonaldense_pb_kernel(tc, x, u_prev, v_last, d, bias, out):
    nc = tc.nc
    with ExitStack() as stack:
        stack.enter_context(tc.manual_schedule())
        const = stack.enter_context(tc.tile_pool(name="const", bufs=1))
        rows_pool = stack.enter_context(tc.tile_pool(name="rows", bufs=U_CHUNKS + X_CHUNKS))
        stage = stack.enter_context(tc.tile_pool(name="stage", bufs=4))
        keep = stack.enter_context(tc.tile_pool(name="keep", bufs=1))
        y_pool = stack.enter_context(tc.tile_pool(name="y", bufs=12))
        psum = stack.enter_context(tc.psum_pool(name="psum", bufs=8))

        v_col = const.tile([P, DIN // P], BF16)
        nc.sync.dma_start(out=v_col[:], in_=v_last.rearrange("(p c) -> p c", p=P))
        v_row = const.tile([P, DIN], BF16)
        nc.gpsimd.memset(v_row[:].bitcast(I32), 0)
        nc.sync.dma_start(out=v_row[0:1, :], in_=v_last.rearrange("(o k) -> o k", o=1))
        d_row = const.tile([P, DOUT], BF16)
        nc.vector.memset(d_row[:].bitcast(I32), 0)
        u_rows = []
        for a in range(U_CHUNKS):
            rows = rows_pool.tile([P, 2, DIN], BF16, tag="rows")
            nc.sync.dma_start(
                out=rows[:],
                in_=u_prev[a * CHUNK : (a + 1) * CHUNK, :].rearrange("(p r) k -> p r k", r=2),
            )
            u_rows.append(rows)
            if a == 1:
                nc.sync.dma_start(out=d_row[0:1, :], in_=d.rearrange("(o j) -> o j", o=1))
        x_rows = []
        for c in range(X_CHUNKS):
            rows = rows_pool.tile([P, 2, DIN], BF16, tag="rows")
            nc.sync.dma_start(
                out=rows[:],
                in_=x[c * CHUNK : (c + 1) * CHUNK, :].rearrange("(p r) k -> p r k", r=2),
            )
            x_rows.append(rows)
            if c == 2:
                bias_bc = const.tile([P, DOUT], BF16)
                nc.sync.dma_start(out=bias_bc[:], in_=bias.partition_broadcast(P))

        minus_half = const.tile([P, P], F32)
        nc.vector.memset(minus_half[:], -0.5)
        warm = const.tile([P, 1], F32)
        nc.scalar.activation(out=warm[:], in_=minus_half[:, 0:1], func=ACT.Square)

        ones_bf16 = const.tile([P, P], BF16)
        nc.vector.memset(ones_bf16[:], 1.0)
        ident = const.tile([P, P], F32)
        make_identity(nc, ident[:])
        eye = const.tile([P, 2, P, 2, PACK], BF16)
        nc.vector.memset(eye[:].rearrange("p u q e t -> p (u q e t)").bitcast(I32), 0)
        eye_pairs = eye[:].rearrange("p u q e t -> p u q (e t)")
        for u in range(2):
            nc.vector.tensor_copy(
                out=eye_pairs[:, u, :, 2 * u : 2 * u + 6 : 5],
                in_=ident[:].unsqueeze(2).to_broadcast([P, P, 2]),
            )
        eye_cols = eye[:].rearrange("p u q e t -> p (u q e) t")
        spot = const.tile([P, 2, CHUNK], BF16)
        nc.gpsimd.memset(spot[:].rearrange("p e c -> p (e c)").bitcast(I32), 0)
        spot_split = spot[:].rearrange("p e (q x) -> p e q x", x=2)
        for e in range(2):
            nc.gpsimd.tensor_scalar(
                out=spot_split[:, e, :, e],
                in0=ident[:],
                scalar1=1.0,
                scalar2=0.0,
                op0=ALU.mult,
                op1=ALU.add,
            )

        u_codes = keep.tile([P, U_CHUNKS, PASSES, CHUNK], U32, align_bytes=64)
        u_scales = keep.tile([P, U_CHUNKS, PASSES, CHUNK], U8, align_bytes=64)
        x_codes = keep.tile([P, X_CHUNKS, PASSES, CHUNK], U32, align_bytes=64)
        x_scales = keep.tile([P, X_CHUNKS, PASSES, CHUNK], U8, align_bytes=64)
        h_codes = keep.tile([P, BLOCKS, PASSES, P], U32, align_bytes=64)
        h_scales = keep.tile([P, BLOCKS, PASSES, P], U8, align_bytes=64)
        w_codes = keep.tile([P, PASSES, DOUT], U32, align_bytes=64)
        w_scales = keep.tile([P, PASSES, DOUT], U8, align_bytes=64)

        def transpose_rows(rows):
            words = rows[:].rearrange("p r k -> p (r k)").bitcast(F32)
            words = words.rearrange("p (r w) -> p r w", r=2)
            grouped = stage.tile([P, PASSES, CHUNK, PACK], BF16, align_bytes=64)
            grouped_words = grouped[:].rearrange("p g c t -> p (g c t)").bitcast(F32)
            grouped_words = grouped_words.rearrange("p (g c u) -> p g c u", g=PASSES, u=2)
            for g in range(PASSES):
                bank = psum.tile([P, 2, CHUNK], F32, tag="bank")
                for u in range(2):
                    first = (2 * g + u) * P
                    for r in range(2):
                        nc.tensor.transpose(
                            bank[:, u, r * P : (r + 1) * P], words[:, r, first : first + P], ident[:]
                        )
                nc.scalar.copy(out=grouped_words[:, g], in_=bank[:].rearrange("p u c -> p c u"))
            return grouped

        def quantise_rows(grouped, codes, scales):
            nc.vector.quantize_mx(
                out=codes.rearrange("p g c -> p (g c)").bitcast(FP8X4),
                scales=scales.rearrange("p g c -> p (g c)"),
                in_=grouped[:].rearrange("p g c t -> p (g c t)"),
            )

        factor = const.tile([P, 1], F32)
        diagonal = const.tile([P, P], F32)
        diagonal_high = const.tile([P, P], BF16)
        diagonal_low = const.tile([P, P], BF16)

        def reflection_factor():
            squares = const.tile([P, DIN // P], F32)
            partial = const.tile([P, 1], F32)
            nc.scalar.activation(out=squares[:], in_=v_col[:], func=ACT.Square, accum_out=partial[:])
            total = psum.tile([P, 1], F32, tag="bank")
            nc.tensor.matmul(out=total[:], lhsT=minus_half[:], rhs=partial[:], start=True, stop=True)
            nc.vector.reciprocal(out=factor[:], in_=total[:])
            inverse = const.tile([P, 1], F32)
            nc.scalar.copy(out=inverse[:], in_=total[:])
            nc.gpsimd.tensor_scalar(
                out=diagonal[:],
                in0=ident[:],
                scalar1=inverse[:, 0:1],
                scalar2=0.0,
                op0=ALU.mult,
                op1=ALU.add,
            )
            nc.gpsimd.tensor_scalar(
                out=diagonal_high[:],
                in0=diagonal[:],
                scalar1=1.0,
                scalar2=0.0,
                op0=ALU.mult,
                op1=ALU.add,
            )
            nc.gpsimd.tensor_tensor(
                out=diagonal_low[:], in0=diagonal[:], in1=diagonal_high[:], op=ALU.subtract
            )

        def spread(row):
            bank = psum.tile([P, DOUT], BF16, tag="bank")
            for half in range(DOUT // N_WIDE):
                cols = slice(half * N_WIDE, (half + 1) * N_WIDE)
                nc.tensor.matmul(
                    out=bank[:, cols], lhsT=ones_bf16[:], rhs=row[:, cols], start=True, stop=True
                )
            return bank

        v_by_word = v_row[:].rearrange("p (g u m e) -> p g u e m", g=PASSES, u=2, e=2)

        def h_products(block):
            cols = slice(block * P, (block + 1) * P)
            h_grouped = stage.tile([P, PASSES, P, PACK], BF16, align_bytes=64)
            for g in range(PASSES):
                bank = psum.tile([P, PACK, P], F32, tag="bank")
                for t in range(PACK):
                    add_here = block >= BLOCKS_PER_SWEEP and 2 * g + t // 2 == block // 2
                    nc.tensor.matmul(
                        out=bank[:, t, :],
                        lhsT=v_by_word[:, g, t // 2, t % 2, :],
                        rhs=v_row[:, cols],
                        start=True,
                        stop=not add_here,
                    )
                    if add_here:
                        place = spot[:, t % 2, (block % 2) * P : (block % 2 + 1) * P]
                        nc.tensor.matmul(
                            out=bank[:, t, :], lhsT=diagonal_high[:], rhs=place, start=False, stop=False
                        )
                        nc.tensor.matmul(
                            out=bank[:, t, :], lhsT=diagonal_low[:], rhs=place, start=False, stop=True
                        )
                products = bank[:].rearrange("p t j -> p j t")
                if block < BLOCKS_PER_SWEEP and g == 0:
                    first = (block % BLOCKS_PER_SWEEP) * P
                    nc.vector.scalar_tensor_tensor(
                        out=h_grouped[:, g],
                        in0=products,
                        scalar=factor[:, 0:1],
                        in1=eye_cols[:, first : first + P, :],
                        op0=ALU.mult,
                        op1=ALU.add,
                    )
                else:
                    nc.scalar.activation(
                        out=h_grouped[:, g], in_=products, func=ACT.Copy, scale=factor[:, 0:1]
                    )
            return h_grouped

        def quantise_h(block, h_grouped):
            nc.vector.quantize_mx(
                out=h_codes[:, block].rearrange("p g j -> p (g j)").bitcast(FP8X4),
                scales=h_scales[:, block].rearrange("p g j -> p (g j)"),
                in_=h_grouped[:].rearrange("p g j t -> p (g j t)"),
            )

        w_halves = {}

        def w_products(block, gi):
            cols = slice(block * P, (block + 1) * P)
            if block % 2 == 0:
                w_pair = stage.tile([P, 2, P, PACK], BF16, align_bytes=64)
                w_halves[block // 2, gi] = w_pair
            bank = psum.tile([P, PACK, P], F32, tag="bank")
            for t in range(PACK):
                chunk = 2 * gi + t // 2
                rows_e = slice((t % 2) * P, (t % 2 + 1) * P)
                for g in range(PASSES):
                    nc.tensor.matmul_mx(
                        out=bank[:, t, :],
                        lhsT=u_codes[:, chunk, g, rows_e].bitcast(FP8X4),
                        lhsT_scale=u_scales[:, chunk, g, rows_e],
                        rhs=h_codes[:, block, g, :].bitcast(FP8X4),
                        rhs_scale=h_scales[:, block, g, :],
                        start=(g == 0),
                        stop=(g == PASSES - 1),
                    )
            nc.vector.tensor_tensor(
                out=w_halves[block // 2, gi][:, block % 2],
                in0=bank[:].rearrange("p t j -> p j t"),
                in1=d_bc[:, cols].unsqueeze(2).to_broadcast([P, P, PACK]),
                op=ALU.mult,
            )

        def quantise_w(pair, gi):
            cols = slice(pair * 2 * P, (pair + 1) * 2 * P)
            nc.vector.quantize_mx(
                out=w_codes[:, gi, cols].bitcast(FP8X4),
                scales=w_scales[:, gi, cols],
                in_=w_halves[pair, gi][:].rearrange("p b j t -> p (b j t)"),
            )

        late_stores = []

        def y_product(sweep, c, r):
            cols = slice(sweep * N_WIDE, (sweep + 1) * N_WIDE)
            rows_r = slice(r * P, (r + 1) * P)
            bank = psum.tile([P, N_WIDE], F32, tag="bank")
            for g in range(PASSES):
                nc.tensor.matmul_mx(
                    out=bank[:],
                    lhsT=x_codes[:, c, g, rows_r].bitcast(FP8X4),
                    lhsT_scale=x_scales[:, c, g, rows_r],
                    rhs=w_codes[:, g, cols].bitcast(FP8X4),
                    rhs_scale=w_scales[:, g, cols],
                    start=(g == 0),
                    stop=(g == PASSES - 1),
                )
            return bank

        def y_rows(c, r):
            return out[c * CHUNK : (c + 1) * CHUNK, :].rearrange("(p r) j -> p r j", r=2)[:, r]

        def y_half(sweep, c, r, through_scalar=False):
            cols = slice(sweep * N_WIDE, (sweep + 1) * N_WIDE)
            bank = y_product(sweep, c, r)
            y_sb = y_pool.tile([P, N_WIDE], F32)
            if through_scalar:
                nc.scalar.copy(out=y_sb[:], in_=bank[:])
                for part in range(2):
                    some = slice(part * N_WIDE // 2, (part + 1) * N_WIDE // 2)
                    biases = bias_bc[:, cols][:, some]
                    nc.gpsimd.tensor_tensor(
                        out=y_sb[:, some], in0=y_sb[:, some], in1=biases, op=ALU.add
                    )
                late_stores.append([3, (y_rows(c, r)[:, cols], y_sb)])
            else:
                nc.vector.tensor_tensor(out=y_sb[:], in0=bank[:], in1=bias_bc[:, cols], op=ALU.add)
                nc.sync.dma_start(out=y_rows(c, r)[:, cols], in_=y_sb[:])
            issue_late()

        def issue_late():
            for late in list(late_stores):
                late[0] = late[0] - 1
                if late[0] == 0:
                    nc.sync.dma_start(out=late[1][0], in_=late[1][1][:])
                    late_stores.remove(late)

        whole_rows = {}

        def y_part(sweep, c, r):
            cols = slice(sweep * N_WIDE, (sweep + 1) * N_WIDE)
            bank = y_product(sweep, c, r)
            if sweep == 0:
                y_whole = y_pool.tile([P, DOUT], F32, bufs=6)
                whole_rows[c, r] = y_whole
            y_whole = whole_rows[c, r]
            nc.vector.tensor_tensor(
                out=y_whole[:, cols], in0=bank[:], in1=bias_bc[:, cols], op=ALU.add
            )
            if sweep == 1:
                nc.sync.dma_start(out=y_rows(c, r), in_=y_whole[:])
            issue_late()

        h_blocks = {}
        grouped_rows = {}

        def make_h(block):
            h_blocks[block] = h_products(block)

        def finish_h(block):
            quantise_h(block, h_blocks[block])

        def turn(kind, c):
            grouped_rows[kind, c] = transpose_rows((u_rows if kind == "u" else x_rows)[c])

        def finish_u(c):
            quantise_rows(grouped_rows["u", c], u_codes[:, c], u_scales[:, c])

        def finish_x(c):
            quantise_rows(grouped_rows["x", c], x_codes[:, c], x_scales[:, c])

        d_bc = const.tile([P, DOUT], BF16)
        reflection_factor()
        make_h(0)
        make_h(1)
        finish_h(0)
        finish_h(1)
        turn("u", 0)
        make_h(2)
        finish_u(0)
        turn("u", 1)
        make_h(3)
        finish_h(2)
        d_bank = spread(d_row)
        turn("u", 2)
        finish_u(1)
        turn("u", 3)
        finish_h(3)
        nc.vector.tensor_copy(out=d_bc[:], in_=d_bank[:])
        w_products(0, 0)
        finish_u(2)
        w_products(1, 0)
        finish_u(3)
        w_products(2, 0)
        quantise_w(0, 0)
        turn("x", 0)
        w_products(3, 0)
        w_products(0, 1)
        quantise_w(1, 0)
        w_products(1, 1)
        turn("x", 1)
        w_products(2, 1)
        quantise_w(0, 1)
        w_products(3, 1)
        finish_x(0)
        make_h(4)
        quantise_w(1, 1)
        turn("x", 2)
        finish_h(4)
        finish_x(1)
        make_h(5)

        for c in range(4):
            later = 4 + c
            y_half(0, c, 0, False)
            w_products(later, 0)
            if c < 3:
                finish_h(later + 1)
            if c == 2:
                quantise_w(2, 1)
            if c < 2:
                finish_x(c + 2)
            if c == 3:
                finish_x(4)
            y_half(0, c, 1, True)
            if c == 0:
                turn("x", 3)
            if c == 2:
                turn("x", 4)
            w_products(later, 1)
            if c % 2 == 1:
                quantise_w(later // 2, 0)
            if c < 2:
                make_h(later + 2)
        quantise_w(3, 1)

        turn("x", 5)
        y_part(0, 4, 0)
        y_part(0, 4, 1)
        y_part(1, 4, 0)
        finish_x(5)
        y_part(1, 4, 1)
        y_half(1, 0, 0, False)
        y_half(1, 0, 1, True)
        turn("x", 6)
        y_part(0, 5, 0)
        y_part(1, 5, 0)
        finish_x(6)
        y_part(0, 5, 1)
        y_part(1, 5, 1)
        y_half(1, 1, 0, True)
        y_half(1, 1, 1, True)
        turn("x", 7)
        y_part(0, 6, 0)
        y_part(1, 6, 0)
        y_part(0, 6, 1)
        finish_x(7)
        y_part(1, 6, 1)
        y_half(1, 2, 0, True)
        y_half(1, 2, 1, False)
        y_half(1, 3, 0, False)
        y_half(1, 3, 1, False)
        y_part(0, 7, 0)
        y_part(1, 7, 0)
        y_part(0, 7, 1)
        y_part(1, 7, 1)
